import numpy as np
import ml_dtypes


def mxq(x, axis, fmt="e4m3"):
    dtype, down = {"e4m3": (ml_dtypes.float8_e4m3fn, 7), "e5m2": (ml_dtypes.float8_e5m2, 14)}[fmt]
    v = np.moveaxis(np.asarray(x, np.float32).astype(ml_dtypes.bfloat16).astype(np.float64), axis, -1)
    blocks = v.reshape(v.shape[:-1] + (-1, 32))
    amax = np.abs(blocks).max(-1, keepdims=True)
    byte = np.maximum(np.where(amax > 0, np.frexp(amax)[1] - 1 + 127, 0) - down, 1)
    scale = np.exp2(byte - 127.0)
    codes = (blocks / scale).astype(np.float32).astype(dtype).astype(np.float64)
    return np.moveaxis((codes * scale).reshape(v.shape), -1, axis)


WIDE = False


def mx_kscale(k):
    if not WIDE:
        return np.ones(k)
    levels = np.array([20, -20, 10, -10, 0])
    a = np.random.permutation(np.resize(levels, k // 512 * 4)).reshape(k // 512, 4)
    idx = np.arange(k)
    return np.exp2(a[idx // 512, idx % 128 // 32])


BF16 = ml_dtypes.bfloat16


def bf(x):
    return np.asarray(x, np.float32).astype(BF16)


def f64(x):
    return np.asarray(x).astype(np.float64)


B, L1, L2, D1, D2, D3 = 4, 512, 512, 1024, 1024, 1024


def setup_inputs():
    u = mx_kscale(D3)
    x1 = np.random.standard_normal((B, L1, D1))
    x2 = np.random.standard_normal((B, L2, D2)) + np.random.standard_normal((B, 1, D2))
    W1 = np.random.standard_normal((D3, D1)) * 0.03 / u[:, None]
    b1 = np.random.standard_normal(D3) * 0.3
    W2 = np.random.standard_normal((D3, D2)) * 0.03
    b2 = np.random.standard_normal(D3) * 0.3
    g = np.random.standard_normal((B, L1, D3)) * np.exp2(np.random.randint(-12, 1, (B, L1, 1))) * 4.0 * u
    return {"x1": bf(x1), "x2": bf(x2), "W1": bf(W1), "b1": bf(b1), "W2": bf(W2), "b2": bf(b2),
            "grad_out": bf(g)}


def reference(x1, x2, W1, b1, W2, b2, grad_out):
    return mxq(f64(grad_out), 2, "e5m2") @ mxq(f64(W1), 0, "e4m3")

@@ -1,0 +1,211 @@
+from contextlib import ExitStack
+
+import concourse.bass as bass
+import concourse.mybir as mybir
+import concourse.tile as tile
+from concourse.masks import make_identity
+
+F32 = mybir.dt.float32
+BF16 = mybir.dt.bfloat16
+U32 = mybir.dt.uint32
+U8 = mybir.dt.uint8
+E4X4 = mybir.dt.float8_e4m3fn_x4
+E5X4 = mybir.dt.float8_e5m2_x4
+
+P = 128
+TOKENS = 2048
+K = 1024
+D = 1024
+NT = TOKENS // P
+NG = K // 512
+NH = D // 512
+
+FLOPS = 2 * TOKENS * K * D
+BYTES = TOKENS * K * 2 + K * D * 2 + TOKENS * D * 4
+
+V_SHARE = 320
+G_CHUNKS = [(0, 2), (2, 4), (4, 8), (8, 16)]
+STORES = [(0, 2), (2, 4), (4, 6), (6, 8), (8, 10), (10, 12), (12, 14), (14, 15), (15, 16)]
+V_OUT = (1, 3)
+
+
+def tile_addpoolingfusion_kernel(tc, x1, x2, W1, b1, W2, b2, grad_out, out):
+    nc = tc.nc
+    g_view = grad_out.flatten_outer_dims().rearrange("(p t) k -> p t k", t=NT)
+    o_view = out.flatten_outer_dims().rearrange("(p t) d -> p t d", t=NT)
+
+    with ExitStack() as ctx:
+        keep = ctx.enter_context(tc.tile_pool(name="keep", bufs=1))
+        psum = ctx.enter_context(tc.psum_pool(name="psum", bufs=1))
+        ctx.enter_context(tc.manual_schedule())
+
+        ident = keep.tile([P, P], F32, name="ident")
+        make_identity(nc, ident[:])
+
+        w_raw = [keep.tile([P, 4, D], BF16, name="w_raw%d" % g) for g in range(NG)]
+        w_grp = [keep.tile([P, D, 4], BF16, name="w_grp%d" % g, align_bytes=64) for g in range(NG)]
+        w_codes = {}
+        w_scales = {}
+        for g in range(NG):
+            for h in range(NH):
+                w_codes[(g, h)] = keep.tile([P, 512], U32, name="w_codes%d%d" % (g, h), align_bytes=64)
+                w_scales[(g, h)] = keep.tile([P, 512], U8, name="w_scales%d%d" % (g, h), align_bytes=64)
+        g_raw = {}
+        for (t0, t1) in G_CHUNKS:
+            chunk = keep.tile([P, t1 - t0, K], BF16, name="g_raw%d" % t0)
+            for t in range(t0, t1):
+                g_raw[t] = (chunk, t - t0)
+        g_grp = [keep.tile([P, 512], F32, name="g_grp%d" % t, align_bytes=64) for t in range(NT)]
+        g_codes = [keep.tile([P, 256], U32, name="g_codes%d" % t, align_bytes=64) for t in range(NT)]
+        g_scales = [keep.tile([P, 256], U8, name="g_scales%d" % t, align_bytes=64) for t in range(NT)]
+        o_sb = {}
+        for (t0, t1) in STORES:
+            o_tile = keep.tile([P, t1 - t0, D], F32, name="o_sb%d" % t0)
+            for t in range(t0, t1):
+                o_sb[t] = (o_tile, t - t0)
+
+        def load_w(g):
+            nc.sync.dma_start(
+                out=w_raw[g][:].rearrange("p (u e) d -> p u (e d)", u=2),
+                in_=W1[512 * g : 512 * g + 512, :].rearrange("(u q e) d -> q u (e d)", u=2, e=2),
+            )
+
+        def load_g(i):
+            t0, t1 = G_CHUNKS[i]
+            nc.sync.dma_start(out=g_raw[t0][0][:], in_=g_view[:, t0:t1, :])
+
+        def regroup(g, h):
+            lo = 512 * h
+            mid = lo + V_SHARE
+            hi = lo + 512
+            nc.vector.tensor_copy(
+                out=w_grp[g][:, lo:mid, :].rearrange("p (c i) t -> p c t i", i=4),
+                in_=w_raw[g][:, :, lo:mid].rearrange("p t (c i) -> p c t i", i=4),
+            )
+            nc.scalar.copy(
+                out=w_grp[g][:, mid:hi, :].rearrange("p (c i) t -> p c t i", i=4),
+                in_=w_raw[g][:, :, mid:hi].rearrange("p t (c i) -> p c t i", i=4),
+            )
+
+        def quant_w(g, h):
+            nc.vector.quantize_mx(
+                out=w_codes[(g, h)][:].bitcast(E4X4),
+                scales=w_scales[(g, h)][:],
+                in_=w_grp[g][:, 512 * h : 512 * h + 512, :].rearrange("p d t -> p (d t)"),
+            )
+
+        banks = {}
+
+        def transposes(t):
+            bank = psum.tile([P, 4, P], F32, name="tp%d" % t, tag="tp%d" % (t % 4))
+            banks[t] = bank
+            chunk, tl = g_raw[t]
+            words = chunk[:, tl, :].bitcast(F32)
+            for c in range(4):
+                nc.tensor.transpose(bank[:, c, :], words[:, P * c : P * c + P], ident[:])
+
+        def evac_t(t, eng):
+            dst = g_grp[t][:].rearrange("p (g r u) -> p g r u", g=2, u=2)
+            src = banks[t][:].rearrange("p (g u) r -> p g r u", u=2)
+            if eng == "v":
+                nc.vector.tensor_copy(out=dst, in_=src)
+            else:
+                nc.scalar.copy(out=dst, in_=src)
+
+        def quant_g(t):
+            nc.vector.quantize_mx(
+                out=g_codes[t][:].bitcast(E5X4),
+                scales=g_scales[t][:],
+                in_=g_grp[t][:].bitcast(BF16),
+            )
+
+        accs = {}
+        order = []
+
+        def mx_pass(t, h, g):
+            if g == 0:
+                idx = len(order)
+                order.append((t, h))
+                accs[(t, h)] = psum.tile([P, 512], F32, name="acc%d_%d" % (t, h), tag="ob%d" % (idx % 4))
+            nc.tensor.matmul_mx(
+                out=accs[(t, h)][:],
+                lhsT=g_codes[t][:, P * g : P * g + P].bitcast(E5X4),
+                lhsT_scale=g_scales[t][:, P * g : P * g + P],
+                rhs=w_codes[(g, h)][:].bitcast(E4X4),
+                rhs_scale=w_scales[(g, h)][:],
+                start=(g == 0),
+                stop=(g == NG - 1),
+            )
+
+        def evac_o(t, h):
+            o_tile, tl = o_sb[t]
+            dst = o_tile[:, tl, 512 * h : 512 * h + 512]
+            if order.index((t, h)) in V_OUT:
+                nc.vector.tensor_copy(out=dst, in_=accs[(t, h)][:])
+            else:
+                nc.scalar.copy(out=dst, in_=accs[(t, h)][:])
+            for (t0, t1) in STORES:
+                if t == t1 - 1 and h == NH - 1:
+                    nc.sync.dma_start(out=o_view[:, t0:t1, :], in_=o_tile[:])
+
+        def product(t):
+            for h in range(NH):
+                for g in range(NG):
+                    mx_pass(t, h, g)
+                evac_o(t, h)
+
+        load_w(0)
+        load_g(0)
+        load_w(1)
+        load_g(1)
+        load_g(2)
+        load_g(3)
+
+        regroup(0, 0)
+        regroup(0, 1)
+        transposes(0)
+        transposes(1)
+        quant_w(0, 0)
+        quant_w(0, 1)
+        evac_t(0, "s")
+        evac_t(1, "s")
+        quant_g(0)
+        quant_g(1)
+        for (t, h) in ((0, 0), (1, 0), (0, 1), (1, 1)):
+            mx_pass(t, h, 0)
+        regroup(1, 0)
+        regroup(1, 1)
+        transposes(2)
+        transposes(3)
+        quant_w(1, 0)
+        quant_w(1, 1)
+        evac_t(2, "s")
+        evac_t(3, "s")
+        quant_g(2)
+        quant_g(3)
+        for (t, h) in ((0, 0), (1, 0), (0, 1), (1, 1)):
+            mx_pass(t, h, 1)
+            evac_o(t, h)
+
+        def next_round(j0):
+            for t in range(j0, j0 + 4):
+                transposes(t)
+            evac_t(j0, "v")
+            evac_t(j0 + 1, "v")
+            quant_g(j0)
+            evac_t(j0 + 2, "v")
+            quant_g(j0 + 1)
+            evac_t(j0 + 3, "v")
+            quant_g(j0 + 2)
+            quant_g(j0 + 3)
+
+        product(2)
+        next_round(4)
+        product(3)
+        for r in range(1, 4):
+            product(4 * r)
+            product(4 * r + 1)
+            if r < 3:
+                next_round(4 * r + 4)
+            product(4 * r + 2)
+            product(4 * r + 3)

@@ -160,6 +160,8 @@ def tile_addpoolingfusion_kernel(tc, x1, x2, W1, b1, W2, b2, grad_out, out):
         load_g(1)
         load_g(2)
         load_g(3)
+        probe = keep.tile([P, 4, K], BF16, name="probe")
+        nc.sync.dma_start(out=probe[:], in_=x1.flatten_outer_dims().rearrange("(p t) k -> p t k", t=NT)[:, 0:4, :])
 
         regroup(0, 0)
         regroup(0, 1)

@@ -48,16 +48,16 @@ def tile_addpoolingfusion_kernel(tc, x1, x2, W1, b1, W2, b2, grad_out, out):
         w_scales = {}
         for g in range(NG):
             for h in range(NH):
-                w_codes[(g, h)] = keep.tile([P, 512], U32, name="w_codes%d%d" % (g, h), align_bytes=64)
-                w_scales[(g, h)] = keep.tile([P, 512], U8, name="w_scales%d%d" % (g, h), align_bytes=64)
+                w_codes[(g, h)] = keep.tile([P, 512], U32, name="w_codes%d%d" % (g, h), align_bytes=256)
+                w_scales[(g, h)] = keep.tile([P, 512], U8, name="w_scales%d%d" % (g, h), align_bytes=256)
         g_raw = {}
         for (t0, t1) in G_CHUNKS:
             chunk = keep.tile([P, t1 - t0, K], BF16, name="g_raw%d" % t0)
             for t in range(t0, t1):
                 g_raw[t] = (chunk, t - t0)
         g_grp = [keep.tile([P, 512], F32, name="g_grp%d" % t, align_bytes=64) for t in range(NT)]
-        g_codes = [keep.tile([P, 256], U32, name="g_codes%d" % t, align_bytes=64) for t in range(NT)]
-        g_scales = [keep.tile([P, 256], U8, name="g_scales%d" % t, align_bytes=64) for t in range(NT)]
+        g_codes = [keep.tile([P, 48 + 256], U32, name="g_codes%d" % t, align_bytes=256) for t in range(NT)]
+        g_scales = [keep.tile([P, 512], U8, name="g_scales%d" % t, align_bytes=256) for t in range(NT)]
         o_sb = {}
         for (t0, t1) in STORES:
             o_tile = keep.tile([P, t1 - t0, D], F32, name="o_sb%d" % t0)
@@ -113,11 +113,12 @@ def tile_addpoolingfusion_kernel(tc, x1, x2, W1, b1, W2, b2, grad_out, out):
                 nc.scalar.copy(out=dst, in_=src)
 
         def quant_g(t):
-            nc.vector.quantize_mx(
-                out=g_codes[t][:].bitcast(E5X4),
-                scales=g_scales[t][:],
-                in_=g_grp[t][:].bitcast(BF16),
-            )
+            for g in range(NG):
+                nc.vector.quantize_mx(
+                    out=g_codes[t][:, 48 + P * g : 48 + P * g + P].bitcast(E5X4),
+                    scales=g_scales[t][:, 256 * g : 256 * g + P],
+                    in_=g_grp[t][:].bitcast(BF16)[:, 512 * g : 512 * g + 512],
+                )
 
         accs = {}
         order = []
@@ -129,8 +130,8 @@ def tile_addpoolingfusion_kernel(tc, x1, x2, W1, b1, W2, b2, grad_out, out):
                 accs[(t, h)] = psum.tile([P, 512], F32, name="acc%d_%d" % (t, h), tag="ob%d" % (idx % 4))
             nc.tensor.matmul_mx(
                 out=accs[(t, h)][:],
-                lhsT=g_codes[t][:, P * g : P * g + P].bitcast(E5X4),
-                lhsT_scale=g_scales[t][:, P * g : P * g + P],
+                lhsT=g_codes[t][:, 48 + P * g : 48 + P * g + P].bitcast(E5X4),
+                lhsT_scale=g_scales[t][:, 256 * g : 256 * g + P],
                 rhs=w_codes[(g, h)][:].bitcast(E4X4),
                 rhs_scale=w_scales[(g, h)][:],
                 start=(g == 0),
@@ -160,8 +161,6 @@ def tile_addpoolingfusion_kernel(tc, x1, x2, W1, b1, W2, b2, grad_out, out):
         load_g(1)
         load_g(2)
         load_g(3)
-        probe = keep.tile([P, 4, K], BF16, name="probe")
-        nc.sync.dma_start(out=probe[:], in_=x1.flatten_outer_dims().rearrange("(p t) k -> p t k", t=NT)[:, 0:4, :])
 
         regroup(0, 0)
         regroup(0, 1)

@@ -155,6 +155,14 @@ def tile_addpoolingfusion_kernel(tc, x1, x2, W1, b1, W2, b2, grad_out, out):
                     mx_pass(t, h, g)
                 evac_o(t, h)
 
+        zeros = keep.tile([P, 512], BF16, name="zeros")
+        nc.vector.memset(zeros[:], 0.0)
+        warm = psum.tile([P, 512], F32, name="warm", tag="ob3")
+
+        def dummy(n, rhs):
+            for i in range(n):
+                nc.tensor.matmul(out=warm[:], lhsT=zeros[:, 0:P], rhs=rhs, start=True, stop=True)
+
         load_w(0)
         load_g(0)
         load_w(1)
@@ -162,10 +170,13 @@ def tile_addpoolingfusion_kernel(tc, x1, x2, W1, b1, W2, b2, grad_out, out):
         load_g(2)
         load_g(3)
 
+        dummy(10, zeros[:])
+        dummy(4, w_raw[0][:, 0, 0:512])
         regroup(0, 0)
         regroup(0, 1)
         transposes(0)
         transposes(1)
+        dummy(2, zeros[:])
         quant_w(0, 0)
         quant_w(0, 1)
         evac_t(0, "s")

@@ -26,7 +26,6 @@ BYTES = TOKENS * K * 2 + K * D * 2 + TOKENS * D * 4
 V_SHARE = 320
 G_CHUNKS = [(0, 2), (2, 4), (4, 8), (8, 16)]
 STORES = [(0, 2), (2, 4), (4, 6), (6, 8), (8, 10), (10, 12), (12, 14), (14, 15), (15, 16)]
-V_OUT = (1, 3)
 
 
 def tile_addpoolingfusion_kernel(tc, x1, x2, W1, b1, W2, b2, grad_out, out):
@@ -141,13 +140,16 @@ def tile_addpoolingfusion_kernel(tc, x1, x2, W1, b1, W2, b2, grad_out, out):
         def evac_o(t, h):
             o_tile, tl = o_sb[t]
             dst = o_tile[:, tl, 512 * h : 512 * h + 512]
-            if order.index((t, h)) in V_OUT:
+            if order.index((t, h)) in (1, 3) or (t >= 12 and h == 0):
                 nc.vector.tensor_copy(out=dst, in_=accs[(t, h)][:])
             else:
                 nc.scalar.copy(out=dst, in_=accs[(t, h)][:])
-            for (t0, t1) in STORES:
-                if t == t1 - 1 and h == NH - 1:
-                    nc.sync.dma_start(out=o_view[:, t0:t1, :], in_=o_tile[:])
+            if t == NT - 1:
+                nc.sync.dma_start(out=o_view[:, t, 512 * h : 512 * h + 512], in_=dst)
+            else:
+                for (t0, t1) in STORES:
+                    if t == t1 - 1 and h == NH - 1:
+                        nc.sync.dma_start(out=o_view[:, t0:t1, :], in_=o_tile[:])
 
         def product(t):
             for h in range(NH):

@@ -172,7 +172,7 @@ def tile_addpoolingfusion_kernel(tc, x1, x2, W1, b1, W2, b2, grad_out, out):
         load_g(2)
         load_g(3)
 
-        dummy(10, zeros[:])
+        dummy(7, zeros[:])
         dummy(4, w_raw[0][:, 0, 0:512])
         regroup(0, 0)
         regroup(0, 1)

@@ -26,6 +26,7 @@ BYTES = TOKENS * K * 2 + K * D * 2 + TOKENS * D * 4
 V_SHARE = 320
 G_CHUNKS = [(0, 2), (2, 4), (4, 8), (8, 16)]
 STORES = [(0, 2), (2, 4), (4, 6), (6, 8), (8, 10), (10, 12), (12, 14), (14, 15), (15, 16)]
+V_OUT = (1, 3)
 
 
 def tile_addpoolingfusion_kernel(tc, x1, x2, W1, b1, W2, b2, grad_out, out):
@@ -47,16 +48,16 @@ def tile_addpoolingfusion_kernel(tc, x1, x2, W1, b1, W2, b2, grad_out, out):
         w_scales = {}
         for g in range(NG):
             for h in range(NH):
-                w_codes[(g, h)] = keep.tile([P, 512], U32, name="w_codes%d%d" % (g, h), align_bytes=256)
-                w_scales[(g, h)] = keep.tile([P, 512], U8, name="w_scales%d%d" % (g, h), align_bytes=256)
+                w_codes[(g, h)] = keep.tile([P, 512], U32, name="w_codes%d%d" % (g, h), align_bytes=64)
+                w_scales[(g, h)] = keep.tile([P, 512], U8, name="w_scales%d%d" % (g, h), align_bytes=64)
         g_raw = {}
         for (t0, t1) in G_CHUNKS:
             chunk = keep.tile([P, t1 - t0, K], BF16, name="g_raw%d" % t0)
             for t in range(t0, t1):
                 g_raw[t] = (chunk, t - t0)
         g_grp = [keep.tile([P, 512], F32, name="g_grp%d" % t, align_bytes=64) for t in range(NT)]
-        g_codes = [keep.tile([P, 48 + 256], U32, name="g_codes%d" % t, align_bytes=256) for t in range(NT)]
-        g_scales = [keep.tile([P, 512], U8, name="g_scales%d" % t, align_bytes=256) for t in range(NT)]
+        g_codes = [keep.tile([P, 256], U32, name="g_codes%d" % t, align_bytes=64) for t in range(NT)]
+        g_scales = [keep.tile([P, 256], U8, name="g_scales%d" % t, align_bytes=64) for t in range(NT)]
         o_sb = {}
         for (t0, t1) in STORES:
             o_tile = keep.tile([P, t1 - t0, D], F32, name="o_sb%d" % t0)
@@ -112,12 +113,11 @@ def tile_addpoolingfusion_kernel(tc, x1, x2, W1, b1, W2, b2, grad_out, out):
                 nc.scalar.copy(out=dst, in_=src)
 
         def quant_g(t):
-            for g in range(NG):
-                nc.vector.quantize_mx(
-                    out=g_codes[t][:, 48 + P * g : 48 + P * g + P].bitcast(E5X4),
-                    scales=g_scales[t][:, 256 * g : 256 * g + P],
-                    in_=g_grp[t][:].bitcast(BF16)[:, 512 * g : 512 * g + 512],
-                )
+            nc.vector.quantize_mx(
+                out=g_codes[t][:].bitcast(E5X4),
+                scales=g_scales[t][:],
+                in_=g_grp[t][:].bitcast(BF16),
+            )
 
         accs = {}
         order = []
@@ -129,8 +129,8 @@ def tile_addpoolingfusion_kernel(tc, x1, x2, W1, b1, W2, b2, grad_out, out):
                 accs[(t, h)] = psum.tile([P, 512], F32, name="acc%d_%d" % (t, h), tag="ob%d" % (idx % 4))
             nc.tensor.matmul_mx(
                 out=accs[(t, h)][:],
-                lhsT=g_codes[t][:, 48 + P * g : 48 + P * g + P].bitcast(E5X4),
-                lhsT_scale=g_scales[t][:, 256 * g : 256 * g + P],
+                lhsT=g_codes[t][:, P * g : P * g + P].bitcast(E5X4),
+                lhsT_scale=g_scales[t][:, P * g : P * g + P],
                 rhs=w_codes[(g, h)][:].bitcast(E4X4),
                 rhs_scale=w_scales[(g, h)][:],
                 start=(g == 0),
@@ -140,16 +140,13 @@ def tile_addpoolingfusion_kernel(tc, x1, x2, W1, b1, W2, b2, grad_out, out):
         def evac_o(t, h):
             o_tile, tl = o_sb[t]
             dst = o_tile[:, tl, 512 * h : 512 * h + 512]
-            if order.index((t, h)) in (1, 3) or (t >= 12 and h == 0):
+            if order.index((t, h)) in V_OUT:
                 nc.vector.tensor_copy(out=dst, in_=accs[(t, h)][:])
             else:
                 nc.scalar.copy(out=dst, in_=accs[(t, h)][:])
-            if t == NT - 1:
-                nc.sync.dma_start(out=o_view[:, t, 512 * h : 512 * h + 512], in_=dst)
-            else:
-                for (t0, t1) in STORES:
-                    if t == t1 - 1 and h == NH - 1:
-                        nc.sync.dma_start(out=o_view[:, t0:t1, :], in_=o_tile[:])
+            for (t0, t1) in STORES:
+                if t == t1 - 1 and h == NH - 1:
+                    nc.sync.dma_start(out=o_view[:, t0:t1, :], in_=o_tile[:])
 
         def product(t):
             for h in range(NH):

from contextlib import ExitStack

import concourse.bass as bass
import concourse.mybir as mybir
import concourse.tile as tile
from concourse.masks import make_identity

F32 = mybir.dt.float32
BF16 = mybir.dt.bfloat16
U32 = mybir.dt.uint32
U8 = mybir.dt.uint8
E4X4 = mybir.dt.float8_e4m3fn_x4
E5X4 = mybir.dt.float8_e5m2_x4

P = 128
TOKENS = 2048
K = 1024
D = 1024
NT = TOKENS // P
NG = K // 512
NH = D // 512

FLOPS = 2 * TOKENS * K * D
BYTES = TOKENS * K * 2 + K * D * 2 + TOKENS * D * 4

V_SHARE = 320
G_CHUNKS = [(0, 2), (2, 4), (4, 8), (8, 16)]
STORES = [(0, 2), (2, 4), (4, 6), (6, 8), (8, 10), (10, 12), (12, 14), (14, 15), (15, 16)]
V_OUT = (1, 3)


def tile_addpoolingfusion_kernel(tc, x1, x2, W1, b1, W2, b2, grad_out, out):
    nc = tc.nc
    g_view = grad_out.flatten_outer_dims().rearrange("(p t) k -> p t k", t=NT)
    o_view = out.flatten_outer_dims().rearrange("(p t) d -> p t d", t=NT)

    with ExitStack() as ctx:
        keep = ctx.enter_context(tc.tile_pool(name="keep", bufs=1))
        psum = ctx.enter_context(tc.psum_pool(name="psum", bufs=1))
        ctx.enter_context(tc.manual_schedule())

        ident = keep.tile([P, P], F32, name="ident")
        make_identity(nc, ident[:])

        w_raw = [keep.tile([P, 4, D], BF16, name="w_raw%d" % g) for g in range(NG)]
        w_grp = [keep.tile([P, D, 4], BF16, name="w_grp%d" % g, align_bytes=64) for g in range(NG)]
        w_codes = {}
        w_scales = {}
        for g in range(NG):
            for h in range(NH):
                w_codes[(g, h)] = keep.tile([P, 512], U32, name="w_codes%d%d" % (g, h), align_bytes=64)
                w_scales[(g, h)] = keep.tile([P, 512], U8, name="w_scales%d%d" % (g, h), align_bytes=64)
        g_raw = {}
        for (t0, t1) in G_CHUNKS:
            chunk = keep.tile([P, t1 - t0, K], BF16, name="g_raw%d" % t0)
            for t in range(t0, t1):
                g_raw[t] = (chunk, t - t0)
        g_grp = [keep.tile([P, 512], F32, name="g_grp%d" % t, align_bytes=64) for t in range(NT)]
        g_codes = [keep.tile([P, 256], U32, name="g_codes%d" % t, align_bytes=64) for t in range(NT)]
        g_scales = [keep.tile([P, 256], U8, name="g_scales%d" % t, align_bytes=64) for t in range(NT)]
        o_sb = {}
        for (t0, t1) in STORES:
            o_tile = keep.tile([P, t1 - t0, D], F32, name="o_sb%d" % t0)
            for t in range(t0, t1):
                o_sb[t] = (o_tile, t - t0)

        def load_w(g):
            nc.sync.dma_start(
                out=w_raw[g][:].rearrange("p (u e) d -> p u (e d)", u=2),
                in_=W1[512 * g : 512 * g + 512, :].rearrange("(u q e) d -> q u (e d)", u=2, e=2),
            )

        def load_g(i):
            t0, t1 = G_CHUNKS[i]
            nc.sync.dma_start(out=g_raw[t0][0][:], in_=g_view[:, t0:t1, :])

        def regroup(g, h):
            lo = 512 * h
            mid = lo + V_SHARE
            hi = lo + 512
            nc.vector.tensor_copy(
                out=w_grp[g][:, lo:mid, :].rearrange("p (c i) t -> p c t i", i=4),
                in_=w_raw[g][:, :, lo:mid].rearrange("p t (c i) -> p c t i", i=4),
            )
            nc.scalar.copy(
                out=w_grp[g][:, mid:hi, :].rearrange("p (c i) t -> p c t i", i=4),
                in_=w_raw[g][:, :, mid:hi].rearrange("p t (c i) -> p c t i", i=4),
            )

        def quant_w(g, h):
            nc.vector.quantize_mx(
                out=w_codes[(g, h)][:].bitcast(E4X4),
                scales=w_scales[(g, h)][:],
                in_=w_grp[g][:, 512 * h : 512 * h + 512, :].rearrange("p d t -> p (d t)"),
            )

        banks = {}

        def transposes(t):
            bank = psum.tile([P, 4, P], F32, name="tp%d" % t, tag="tp%d" % (t % 4))
            banks[t] = bank
            chunk, tl = g_raw[t]
            words = chunk[:, tl, :].bitcast(F32)
            for c in range(4):
                nc.tensor.transpose(bank[:, c, :], words[:, P * c : P * c + P], ident[:])

        def evac_t(t, eng):
            dst = g_grp[t][:].rearrange("p (g r u) -> p g r u", g=2, u=2)
            src = banks[t][:].rearrange("p (g u) r -> p g r u", u=2)
            if eng == "v":
                nc.vector.tensor_copy(out=dst, in_=src)
            else:
                nc.scalar.copy(out=dst, in_=src)

        def quant_g(t):
            nc.vector.quantize_mx(
                out=g_codes[t][:].bitcast(E5X4),
                scales=g_scales[t][:],
                in_=g_grp[t][:].bitcast(BF16),
            )

        accs = {}
        order = []

        def mx_pass(t, h, g):
            if g == 0:
                idx = len(order)
                order.append((t, h))
                accs[(t, h)] = psum.tile([P, 512], F32, name="acc%d_%d" % (t, h), tag="ob%d" % (idx % 4))
            nc.tensor.matmul_mx(
                out=accs[(t, h)][:],
                lhsT=g_codes[t][:, P * g : P * g + P].bitcast(E5X4),
                lhsT_scale=g_scales[t][:, P * g : P * g + P],
                rhs=w_codes[(g, h)][:].bitcast(E4X4),
                rhs_scale=w_scales[(g, h)][:],
                start=(g == 0),
                stop=(g == NG - 1),
            )

        def evac_o(t, h):
            o_tile, tl = o_sb[t]
            dst = o_tile[:, tl, 512 * h : 512 * h + 512]
            if order.index((t, h)) in V_OUT:
                nc.vector.tensor_copy(out=dst, in_=accs[(t, h)][:])
            else:
                nc.scalar.copy(out=dst, in_=accs[(t, h)][:])
            for (t0, t1) in STORES:
                if t == t1 - 1 and h == NH - 1:
                    nc.sync.dma_start(out=o_view[:, t0:t1, :], in_=o_tile[:])

        def product(t):
            for h in range(NH):
                for g in range(NG):
                    mx_pass(t, h, g)
                evac_o(t, h)

        zeros = keep.tile([P, 512], BF16, name="zeros")
        nc.vector.memset(zeros[:], 0.0)
        warm = psum.tile([P, 512], F32, name="warm", tag="ob3")

        def dummy(n, rhs):
            for i in range(n):
                nc.tensor.matmul(out=warm[:], lhsT=zeros[:, 0:P], rhs=rhs, start=True, stop=True)

        load_w(0)
        load_g(0)
        load_w(1)
        load_g(1)
        load_g(2)
        load_g(3)

        dummy(7, zeros[:])
        dummy(4, w_raw[0][:, 0, 0:512])
        regroup(0, 0)
        regroup(0, 1)
        transposes(0)
        transposes(1)
        dummy(2, zeros[:])
        quant_w(0, 0)
        quant_w(0, 1)
        evac_t(0, "s")
        evac_t(1, "s")
        quant_g(0)
        quant_g(1)
        for (t, h) in ((0, 0), (1, 0), (0, 1), (1, 1)):
            mx_pass(t, h, 0)
        regroup(1, 0)
        regroup(1, 1)
        transposes(2)
        transposes(3)
        quant_w(1, 0)
        quant_w(1, 1)
        evac_t(2, "s")
        evac_t(3, "s")
        quant_g(2)
        quant_g(3)
        for (t, h) in ((0, 0), (1, 0), (0, 1), (1, 1)):
            mx_pass(t, h, 1)
            evac_o(t, h)

        def next_round(j0):
            for t in range(j0, j0 + 4):
                transposes(t)
            evac_t(j0, "v")
            evac_t(j0 + 1, "v")
            quant_g(j0)
            evac_t(j0 + 2, "v")
            quant_g(j0 + 1)
            evac_t(j0 + 3, "v")
            quant_g(j0 + 2)
            quant_g(j0 + 3)

        product(2)
        next_round(4)
        product(3)
        for r in range(1, 4):
            product(4 * r)
            product(4 * r + 1)
            if r < 3:
                next_round(4 * r + 4)
            product(4 * r + 2)
            product(4 * r + 3)
